import numpy as np
import ml_dtypes


def mxq(x, axis, fmt="e4m3"):
    dtype, down = {"e4m3": (ml_dtypes.float8_e4m3fn, 7), "e5m2": (ml_dtypes.float8_e5m2, 14)}[fmt]
    v = np.moveaxis(np.asarray(x, np.float32).astype(ml_dtypes.bfloat16).astype(np.float64), axis, -1)
    blocks = v.reshape(v.shape[:-1] + (-1, 32))
    amax = np.abs(blocks).max(-1, keepdims=True)
    byte = np.maximum(np.where(amax > 0, np.frexp(amax)[1] - 1 + 127, 0) - down, 1)
    scale = np.exp2(byte - 127.0)
    codes = (blocks / scale).astype(np.float32).astype(dtype).astype(np.float64)
    return np.moveaxis((codes * scale).reshape(v.shape), -1, axis)


WIDE = False


def mx_kscale(k, group=512):
    if not WIDE:
        return np.ones(k)
    levels = np.array([10, -10, 5, -5, 0])
    if group != 512:
        return np.exp2(np.random.permutation(np.resize(levels, k // group))).repeat(group)
    if k % 512:
        return np.exp2(np.random.permutation(np.resize(levels, k // 32))).repeat(32)
    a = np.empty((k // 512, 16))
    for p in range(k // 512):
        a[p, :8] = np.random.permutation(np.resize(levels, 8))
        for g in range(8):
            far = levels[np.abs(levels - a[p, g]) >= 10]
            a[p, g + 8] = far[np.random.randint(len(far))]
    return np.exp2(a.ravel()).repeat(32)


BF16 = ml_dtypes.bfloat16


def bf(x):
    return np.asarray(x, np.float32).astype(BF16)


def f64(x):
    return np.asarray(x).astype(np.float64)


B, H, W, C, NS = 2, 2, 1024, 512, 2
WIN = W // NS
SHIFT = WIN // 2


def windows(x, b, h, w, n):
    x = f64(x)
    c = x.shape[-1]
    x = np.roll(x.reshape(b * h, w, c), -(w // n // 2), axis=1)
    return x.reshape(b * h, n, w // n, c)


def unwindows(x, b, h, w, n):
    c = x.shape[-1]
    x = np.roll(x.reshape(b * h, w, c), w // n // 2, axis=1)
    return x.reshape(b, h * w, c)


def setup_inputs():
    s = mx_kscale(WIN, 128)
    u = mx_kscale(C, 128)
    q = bf(np.random.standard_normal((B, H * W, C)))
    k = bf(np.random.standard_normal((B, H * W, C)))
    v0 = bf(np.random.standard_normal((B, H * W, C)) * 2.0)
    m0 = bf(np.random.standard_normal((NS, WIN, WIN)))
    g = bf(np.random.standard_normal((B, H * W, C)) * np.exp2(np.random.randint(-6, 1, (B, H * W, 1))) * 16.0 * u)
    scores = windows(q, B, H, W, NS) @ windows(k, B, H, W, NS).transpose(0, 1, 3, 2) / C ** 0.5
    row_max = (scores + f64(m0)[None]).max(-1)
    return {"q": q, "k": k,
            "v": bf(f64(v0) / u),
            "attn_mask": bf(f64(m0) + np.log(s)[None, :, None]),
            "h": H, "w": W, "num_splits": NS,
            "scores": np.asarray(scores, np.float32),
            "row_max": np.asarray(row_max, np.float32),
            "grad_out": g}


def reference(q, k, v, attn_mask, h, w, num_splits, scores, row_max, grad_out):
    b = v.shape[0]
    vs = windows(v, b, h, w, num_splits)
    gs = windows(grad_out, b, h, w, num_splits)
    e = np.exp(f64(scores) + f64(attn_mask)[None] - f64(row_max)[..., None])
    z = e.sum(-1, keepdims=True)
    dz = gs / z
    dvs = mxq(e, 2, "e4m3").transpose(0, 1, 3, 2) @ mxq(dz, 2, "e5m2")
    de = mxq(dz, 3, "e5m2") @ mxq(vs, 3, "e4m3").transpose(0, 1, 3, 2)
    ds = e * (de - (e * de).sum(-1, keepdims=True) / z)
    return unwindows(dvs, b, h, w, num_splits), ds.sum(0)

@@ -1,0 +1,336 @@
+from contextlib import ExitStack
+
+import concourse.mybir as mybir
+from concourse.masks import make_identity
+
+F32 = mybir.dt.float32
+BF16 = mybir.dt.bfloat16
+U32 = mybir.dt.uint32
+U8 = mybir.dt.uint8
+E4M3X4 = mybir.dt.float8_e4m3fn_x4
+E5M2X4 = mybir.dt.float8_e5m2_x4
+ADD = mybir.AluOpType.add
+MULT = mybir.AluOpType.mult
+EXP = mybir.ActivationFunctionType.Exp
+
+P = 128
+J = 4
+WIN = 512
+C = 512
+ROWS = 4
+SPLITS = 2
+
+FLOPS = 2 * ROWS * SPLITS * 2 * WIN * WIN * C
+BYTES = 4 * ROWS * SPLITS * WIN * WIN + 2 * 2 * (ROWS * SPLITS * WIN * C) + 2 * SPLITS * WIN * WIN + 4 * ROWS * SPLITS * WIN * C + 4 * SPLITS * WIN * WIN
+
+PE_SUMMED = ((0, 0), (0, 1), (1, 0))
+E_COLS_ON_VECTOR = 128
+
+WORDS_ON_VECTOR = ()
+
+
+def tile_single_head_split_window_attention_1d_v_kernel(
+    tc, q, k, v, attn_mask, h, w, num_splits, scores, row_max, grad_out, out_0, out_1
+):
+    nc = tc.nc
+    assert (w, num_splits) == (SPLITS * WIN, SPLITS)
+    steps = [(n, r) for n in range(SPLITS) for r in range(ROWS)]
+    last = len(steps) - 1
+
+    with ExitStack() as ctx:
+        keep = ctx.enter_context(tc.tile_pool(name="keep", bufs=1))
+        io = ctx.enter_context(tc.tile_pool(name="io", bufs=1))
+        work = ctx.enter_context(tc.tile_pool(name="work", bufs=2))
+        small = ctx.enter_context(tc.tile_pool(name="small", bufs=4))
+        psum = ctx.enter_context(tc.psum_pool(name="psum", bufs=1))
+
+        ident = keep.tile([P, P], F32, name="ident")
+        warm = keep.tile([P, 1], F32, name="warm")
+        rmax = keep.tile([P, len(steps), 2 * J], F32, name="rmax")
+        neg_max = keep.tile([P, len(steps), J], F32, name="neg_max")
+        mask = [keep.tile([P, J, WIN], BF16, name="mask%d" % n) for n in range(SPLITS)]
+        acc = [keep.tile([P, J, WIN], F32, name="acc%d" % n) for n in range(SPLITS)]
+        tiles = [dict() for s in steps]
+        sums = {}
+
+        def image(x, r):
+            return x[r // h]
+
+        def spans(n, r):
+            first = (r % h) * w
+            start = n * WIN + WIN // 2
+            if start + WIN <= w:
+                return [(0, first + start, WIN)]
+            head = w - start
+            return [(0, first + start, head), (head, first, WIN - head)]
+
+        def load_scores(i, halves):
+            n, r = steps[i]
+            t = io.tile([P, J, WIN], F32, name="e", bufs=6)
+            tiles[i]["e"] = t
+            src = scores[r, n].rearrange("(p j) k -> p j k", j=J)
+            for a in range(0, J, J // halves):
+                nc.sync.dma_start(out=t[:, a : a + J // halves, :], in_=src[:, a : a + J // halves, :])
+                if r == 0:
+                    msrc = attn_mask[n].rearrange("(p j) k -> p j k", j=J)
+                    nc.sync.dma_start(out=mask[n][:, a : a + J // halves, :], in_=msrc[:, a : a + J // halves, :])
+
+        def late_scores(i):
+            if i > 5:
+                load_scores(i, 1)
+
+        def load_grad(i):
+            n, r = steps[i]
+            t = io.tile([P, J, C], BF16, name="g", bufs=8)
+            tiles[i]["g"] = t
+            for win0, x0, rows in spans(n, r):
+                src = image(grad_out, r)[x0 : x0 + rows, :].rearrange("(p j) c -> p j c", j=J)
+                nc.sync.dma_start(out=t[win0 // J : (win0 + rows) // J, :, :], in_=src)
+
+        def load_v(i):
+            n, r = steps[i]
+            t = io.tile([P, J, C], BF16, name="v", bufs=8)
+            tiles[i]["v"] = t
+            for win0, x0, rows in spans(n, r):
+                src = image(v, r)[x0 : x0 + rows, :].rearrange("(t p) c -> p t c", p=P)
+                nc.sync.dma_start(out=t[:, win0 // P : (win0 + rows) // P, :], in_=src)
+
+        def add_mask(i, half):
+            e = tiles[i]["e"]
+            sl = slice(2 * half, 2 * half + 2)
+            nc.vector.tensor_tensor(out=e[:, sl, :], in0=e[:, sl, :], in1=mask[steps[i][0]][:, sl, :], op=ADD)
+
+        def exponential(i, j):
+            if j == 0:
+                tiles[i]["z"] = small.tile([P, J], F32, name="z")
+            e = tiles[i]["e"]
+            nc.scalar.activation(
+                out=e[:, j, :], in_=e[:, j, :], func=EXP, bias=neg_max[:, i, j : j + 1], accum_out=tiles[i]["z"][:, j : j + 1]
+            )
+
+        def invert(i):
+            tiles[i]["rz"] = small.tile([P, J], F32, name="rz")
+            nc.vector.reciprocal(out=tiles[i]["rz"][:], in_=tiles[i]["z"][:])
+
+        def scale(i):
+            tiles[i]["dz"] = work.tile([P, J, C], BF16, name="dz", align_bytes=64)
+            for j in range(J):
+                nc.vector.tensor_scalar(
+                    out=tiles[i]["dz"][:, j, :], in0=tiles[i]["g"][:, j, :], scalar1=tiles[i]["rz"][:, j : j + 1], scalar2=None, op0=MULT
+                )
+
+        def four_by_four(dst, src, cols):
+            return dict(
+                out=dst[:, cols, :].rearrange("p (c i) j -> p c j i", i=4),
+                in_=src[:, :, cols].rearrange("p j (c i) -> p c j i", i=4),
+            )
+
+        def interleave_e_v(i):
+            tiles[i]["e_il"] = work.tile([P, WIN, J], BF16, name="e_il", align_bytes=64)
+            if E_COLS_ON_VECTOR:
+                nc.vector.tensor_copy(**four_by_four(tiles[i]["e_il"], tiles[i]["e"], slice(0, E_COLS_ON_VECTOR)))
+
+        def interleave_e_s(i):
+            nc.scalar.copy(**four_by_four(tiles[i]["e_il"], tiles[i]["e"], slice(E_COLS_ON_VECTOR, WIN)))
+
+        def interleave_dz(i):
+            tiles[i]["dz_il"] = work.tile([P, C, J], BF16, name="dz_il", align_bytes=64)
+            nc.scalar.copy(**four_by_four(tiles[i]["dz_il"], tiles[i]["dz"], slice(0, C)))
+
+        def quantise(i, name, src, fmt):
+            codes = work.tile([P, 512], U32, name=name + "_q", align_bytes=64)
+            scl = work.tile([P, 512], U8, name=name + "_s", align_bytes=64)
+            tiles[i][name + "_q"] = codes[:].bitcast(fmt)
+            tiles[i][name + "_s"] = scl
+            nc.vector.quantize_mx(out=codes[:].bitcast(fmt), scales=scl[:], in_=tiles[i][src][:].rearrange("p a b -> p (a b)"))
+
+        def turn(i, name, b):
+            words = tiles[i][name][:].rearrange("p a c -> p (a c)").bitcast(F32).rearrange("p (a c) -> p a c", a=J)
+            ps = psum.tile([P, 2, 2, P], F32, name="turn", bufs=2)
+            tiles[i][name, b] = ps
+            for a in range(2):
+                for u in range(2):
+                    nc.tensor.transpose(ps[:, a, u, :], words[:, 2 * b + a, u : C // 2 : 2], ident[:])
+
+        def unload(i, name, b):
+            if b == 0:
+                tiles[i][name + "_t"] = work.tile([P, WIN, J], BF16, name=name + "_t", align_bytes=64)
+            words = tiles[i][name + "_t"][:].rearrange("p x j -> p (x j)").bitcast(F32)
+            words = words.rearrange("p (b a x u) -> p b a x u", b=2, a=2, u=2)
+            src = tiles[i][name, b][:].rearrange("p a u x -> p a x u")
+            if (name, b) in WORDS_ON_VECTOR:
+                nc.vector.tensor_copy(out=words[:, b], in_=src)
+            else:
+                nc.scalar.copy(out=words[:, b], in_=src)
+
+        def multiply_de(i, j):
+            t = tiles[i]
+            ps = psum.tile([P, WIN], F32, name="de", bufs=2)
+            t["de", j] = ps
+            cols = slice(P * j, P * (j + 1))
+            nc.tensor.matmul_mx(
+                out=ps[:], lhsT=t["dzt_q"][:, cols], lhsT_scale=t["dzt_s"][:, cols], rhs=t["vt_q"], rhs_scale=t["vt_s"][:],
+                start=True, stop=True,
+            )
+
+        def multiply_dv(i, m):
+            t = tiles[i]
+            ps = psum.tile([P, C], F32, name="dv", bufs=2)
+            t["dv", m] = ps
+            cols = slice(P * m, P * (m + 1))
+            nc.tensor.matmul_mx(
+                out=ps[:], lhsT=t["e_q"][:, cols], lhsT_scale=t["e_s"][:, cols], rhs=t["dz_q"], rhs_scale=t["dz_s"][:],
+                start=True, stop=True,
+            )
+
+        def empty_dv(i, m):
+            n, r = steps[i]
+            if m == 0:
+                tiles[i]["dv_sb"] = work.tile([P, J, C], F32, name="dv_sb")
+            sb = tiles[i]["dv_sb"]
+            nc.scalar.copy(out=sb[:, m, :], in_=tiles[i]["dv", m][:])
+            if m % 2:
+                x0 = [x0 + P * (m - 1) - win0 for win0, x0, rows in spans(n, r) if win0 <= P * (m - 1) < win0 + rows][0]
+                dst = image(out_0, r)[x0 : x0 + 2 * P, :].rearrange("(t p) c -> p t c", p=P)
+                nc.sync.dma_start(out=dst, in_=sb[:, m - 1 : m + 1, :])
+
+        def weigh(i, j):
+            if j == 0:
+                tiles[i]["prod"] = work.tile([P, J, WIN], F32, name="prod")
+                tiles[i]["dot"] = small.tile([P, J], F32, name="dot")
+            t = tiles[i]
+            nc.vector.scalar_tensor_tensor(
+                out=t["prod"][:, j, :], in0=t["de", j][:], scalar=1.0, in1=t["e"][:, j, :], op0=MULT, op1=MULT,
+                accum_out=t["dot"][:, j : j + 1],
+            )
+
+        def factors(i):
+            t = tiles[i]
+            t["factor"] = small.tile([P, J], F32, name="factor")
+            nc.vector.scalar_tensor_tensor(out=t["factor"][:], in0=t["dot"][:], scalar=-1.0, in1=t["rz"][:], op0=MULT, op1=MULT)
+
+        def diagonals(i):
+            t = tiles[i]
+            for j in range(J):
+                if (steps[i][0], j) in PE_SUMMED:
+                    t["diag", j] = small.tile([P, P], F32, name="diag", bufs=4)
+                    nc.gpsimd.tensor_scalar(out=t["diag", j][:], in0=ident[:], scalar1=t["factor"][:, j : j + 1], scalar2=0.0, op0=MULT, op1=ADD)
+
+        def sum_on_tensor(i, j):
+            n, r = steps[i]
+            t = tiles[i]
+            if (n, j) in PE_SUMMED:
+                if r == 0:
+                    sums[n, j] = psum.tile([P, WIN], F32, name="sum", bufs=2)
+                nc.tensor.matmul(out=sums[n, j][:], lhsT=ident[:], rhs=t["prod"][:, j, :], start=(r == 0), stop=False)
+                nc.tensor.matmul(out=sums[n, j][:], lhsT=t["diag", j][:], rhs=t["e"][:, j, :], start=False, stop=(r == ROWS - 1))
+
+        def subtract(i, j):
+            n, r = steps[i]
+            t = tiles[i]
+            if (n, j) not in PE_SUMMED:
+                dst = acc[n] if r == 0 else t["prod"]
+                nc.vector.scalar_tensor_tensor(
+                    out=dst[:, j, :], in0=t["e"][:, j, :], scalar=t["factor"][:, j : j + 1], in1=t["prod"][:, j, :], op0=MULT, op1=ADD
+                )
+
+        def accumulate(i, a, b):
+            n, r = steps[i]
+            mine = [j for j in range(a, b) if (n, j) not in PE_SUMMED]
+            if r > 0 and mine:
+                sl = slice(mine[0], b)
+                nc.vector.tensor_tensor(out=acc[n][:, sl, :], in0=acc[n][:, sl, :], in1=tiles[i]["prod"][:, sl, :], op=ADD)
+                if r == ROWS - 1:
+                    store_sum(n, sl)
+
+        def store_sum(n, sl):
+            nc.sync.dma_start(out=out_1[n].rearrange("(p j) k -> p j k", j=J)[:, sl, :], in_=acc[n][:, sl, :])
+
+        def empty_sum(i, j):
+            n, r = steps[i]
+            if r == ROWS - 1 and (n, j) in PE_SUMMED:
+                nc.scalar.copy(out=acc[n][:, j, :], in_=sums[n, j][:])
+                store_sum(n, slice(j, j + 1))
+
+        make_identity(nc, ident[:])
+        nc.vector.memset(warm[:], 0.0)
+        nc.scalar.activation(out=warm[:], in_=warm[:], func=EXP)
+        with tc.manual_schedule():
+            for a, b in ((0, 1), (1, 4), (4, 5), (5, 8)):
+                n, r0 = steps[a]
+                src = row_max[r0 : r0 + b - a, n].rearrange("r (p j) -> p r j", j=J)
+                nc.scalar.dma_start(out=rmax[:, a:b, 0:J], in_=src)
+            for a, b in ((0, 1), (1, 8)):
+                nc.gpsimd.tensor_scalar(out=neg_max[:, a:b, :], in0=rmax[:, a:b, 0:J], scalar1=-1.0, scalar2=0.0, op0=MULT, op1=ADD)
+            load_scores(0, 2)
+            load_grad(0)
+            load_v(0)
+            load_scores(1, 1)
+            load_grad(1)
+            load_v(1)
+            for i in range(2, 6):
+                load_scores(i, 1)
+                load_grad(i)
+                load_v(i)
+            for i in range(6, 8):
+                load_grad(i)
+                load_v(i)
+
+            order = (
+                (subtract, -2, 1),
+                (quantise, -1, "dzt", "dz_t", E5M2X4),
+                (multiply_de, -1, 0),
+                (diagonals, -2),
+                (multiply_dv, -2, 2),
+                (empty_dv, -2, 2),
+                (subtract, -2, 2),
+                (multiply_dv, -2, 3),
+                (empty_dv, -2, 3),
+                (add_mask, 1, 0),
+                (multiply_de, -1, 1),
+                (accumulate, -2, 0, 2),
+                (sum_on_tensor, -2, 0),
+                (late_scores, 3),
+                (weigh, -1, 0),
+                (empty_sum, -2, 0),
+                (subtract, -3, 0),
+                (quantise, -1, "e", "e_il", E4M3X4),
+                (accumulate, -2, 2, 4),
+                (unload, 0, "v", 0),
+                (quantise, -1, "dz", "dz_il", E5M2X4),
+                (multiply_de, -1, 3),
+                (invert, 0),
+                (weigh, -1, 1),
+                (multiply_dv, -1, 0),
+                (multiply_dv, -1, 1),
+                (scale, 0),
+                (unload, 0, "v", 1),
+                (interleave_e_v, 0),
+                (interleave_e_s, 0),
+                (weigh, -1, 3),
+                (multiply_de, -1, 2),
+                (exponential, 1, 0),
+                (turn, 0, "dz", 0),
+                (exponential, 1, 1),
+                (add_mask, 1, 1),
+                (turn, 0, "dz", 1),
+                (unload, 0, "dz", 0),
+                (unload, 0, "dz", 1),
+                (sum_on_tensor, -2, 1),
+                (empty_sum, -3, 1),
+                (weigh, -1, 2),
+                (quantise, 0, "vt", "v_t", E4M3X4),
+                (turn, 1, "v", 0),
+                (exponential, 1, 2),
+                (empty_dv, -1, 0),
+                (empty_dv, -1, 1),
+                (interleave_dz, 0),
+                (turn, 1, "v", 1),
+                (factors, -1),
+                (exponential, 1, 3),
+                (subtract, -1, 3),
+            )
+            for t in range(-2, last + 3):
+                for op, ahead, *args in order:
+                    if 0 <= t + ahead <= last:
+                        op(t + ahead, *args)

@@ -24,8 +24,11 @@ FLOPS = 2 * ROWS * SPLITS * 2 * WIN * WIN * C
 BYTES = 4 * ROWS * SPLITS * WIN * WIN + 2 * 2 * (ROWS * SPLITS * WIN * C) + 2 * SPLITS * WIN * WIN + 4 * ROWS * SPLITS * WIN * C + 4 * SPLITS * WIN * WIN
 
 PE_SUMMED = ((0, 0), (0, 1), (1, 0))
-E_COLS_ON_VECTOR = 128
+E_COLS_ON_VECTOR = 256
 
+TURN_BUFS, DE_BUFS, DV_BUFS = 2, 2, 2
+G_FROM = 2
+G_HALF = 1
 WORDS_ON_VECTOR = ()
 
 
@@ -98,7 +101,9 @@ def tile_single_head_split_window_attention_1d_v_kernel(
         def add_mask(i, half):
             e = tiles[i]["e"]
             sl = slice(2 * half, 2 * half + 2)
-            nc.vector.tensor_tensor(out=e[:, sl, :], in0=e[:, sl, :], in1=mask[steps[i][0]][:, sl, :], op=ADD)
+            for js in [sl] if i < G_FROM or half < G_HALF else [slice(j, j + 1) for j in range(2 * half, 2 * half + 2)]:
+                engine = nc.vector if i < G_FROM or half < G_HALF else nc.gpsimd
+                engine.tensor_tensor(out=e[:, js, :], in0=e[:, js, :], in1=mask[steps[i][0]][:, js, :], op=ADD)
 
         def exponential(i, j):
             if j == 0:
@@ -146,7 +151,7 @@ def tile_single_head_split_window_attention_1d_v_kernel(
 
         def turn(i, name, b):
             words = tiles[i][name][:].rearrange("p a c -> p (a c)").bitcast(F32).rearrange("p (a c) -> p a c", a=J)
-            ps = psum.tile([P, 2, 2, P], F32, name="turn", bufs=2)
+            ps = psum.tile([P, 2, 2, P], F32, name="turn", bufs=TURN_BUFS)
             tiles[i][name, b] = ps
             for a in range(2):
                 for u in range(2):
@@ -165,7 +170,7 @@ def tile_single_head_split_window_attention_1d_v_kernel(
 
         def multiply_de(i, j):
             t = tiles[i]
-            ps = psum.tile([P, WIN], F32, name="de", bufs=2)
+            ps = psum.tile([P, WIN], F32, name="de", bufs=DE_BUFS)
             t["de", j] = ps
             cols = slice(P * j, P * (j + 1))
             nc.tensor.matmul_mx(
@@ -175,7 +180,7 @@ def tile_single_head_split_window_attention_1d_v_kernel(
 
         def multiply_dv(i, m):
             t = tiles[i]
-            ps = psum.tile([P, C], F32, name="dv", bufs=2)
+            ps = psum.tile([P, C], F32, name="dv", bufs=DV_BUFS)
             t["dv", m] = ps
             cols = slice(P * m, P * (m + 1))
             nc.tensor.matmul_mx(
@@ -277,60 +282,60 @@ def tile_single_head_split_window_attention_1d_v_kernel(
                 load_v(i)
 
             order = (
-                (subtract, -2, 1),
                 (quantise, -1, "dzt", "dz_t", E5M2X4),
                 (multiply_de, -1, 0),
-                (diagonals, -2),
+                (subtract, -2, 3),
                 (multiply_dv, -2, 2),
-                (empty_dv, -2, 2),
-                (subtract, -2, 2),
                 (multiply_dv, -2, 3),
-                (empty_dv, -2, 3),
-                (add_mask, 1, 0),
-                (multiply_de, -1, 1),
-                (accumulate, -2, 0, 2),
-                (sum_on_tensor, -2, 0),
-                (late_scores, 3),
-                (weigh, -1, 0),
-                (empty_sum, -2, 0),
-                (subtract, -3, 0),
-                (quantise, -1, "e", "e_il", E4M3X4),
-                (accumulate, -2, 2, 4),
-                (unload, 0, "v", 0),
-                (quantise, -1, "dz", "dz_il", E5M2X4),
-                (multiply_de, -1, 3),
-                (invert, 0),
-                (weigh, -1, 1),
-                (multiply_dv, -1, 0),
-                (multiply_dv, -1, 1),
-                (scale, 0),
-                (unload, 0, "v", 1),
+                (subtract, -2, 0),
+                (interleave_dz, -1),
                 (interleave_e_v, 0),
+                (multiply_de, -1, 1),
+                (empty_dv, -2, 2),
+                (invert, 0),
+                (unload, 0, "v", 0),
+                (empty_dv, -2, 3),
+                (sum_on_tensor, -2, 0),
+                (accumulate, -2, 0, 2),
+                (empty_sum, -2, 0),
+                (unload, 0, "v", 1),
+                (accumulate, -2, 2, 4),
+                (add_mask, 1, 0),
+                (weigh, -1, 0),
+                (multiply_de, -1, 3),
                 (interleave_e_s, 0),
-                (weigh, -1, 3),
-                (multiply_de, -1, 2),
+                (quantise, -1, "dz", "dz_il", E5M2X4),
+                (weigh, -1, 1),
+                (scale, 0),
+                (multiply_dv, -1, 0),
                 (exponential, 1, 0),
+                (multiply_de, -1, 2),
                 (turn, 0, "dz", 0),
                 (exponential, 1, 1),
-                (add_mask, 1, 1),
-                (turn, 0, "dz", 1),
+                (weigh, -1, 3),
                 (unload, 0, "dz", 0),
-                (unload, 0, "dz", 1),
-                (sum_on_tensor, -2, 1),
-                (empty_sum, -3, 1),
                 (weigh, -1, 2),
+                (late_scores, 2),
+                (add_mask, 1, 1),
+                (exponential, 1, 3),
+                (turn, 0, "dz", 1),
+                (multiply_dv, -1, 1),
+                (sum_on_tensor, -2, 1),
                 (quantise, 0, "vt", "v_t", E4M3X4),
                 (turn, 1, "v", 0),
-                (exponential, 1, 2),
-                (empty_dv, -1, 0),
-                (empty_dv, -1, 1),
-                (interleave_dz, 0),
+                (unload, 0, "dz", 1),
                 (turn, 1, "v", 1),
                 (factors, -1),
-                (exponential, 1, 3),
-                (subtract, -1, 3),
+                (exponential, 1, 2),
+                (quantise, 0, "e", "e_il", E4M3X4),
+                (empty_dv, -1, 0),
+                (subtract, -1, 1),
+                (diagonals, -1),
+                (empty_sum, -3, 1),
+                (subtract, -1, 2),
+                (empty_dv, -1, 1),
             )
-            for t in range(-2, last + 3):
+            for t in range(-3, last + 4):
                 for op, ahead, *args in order:
                     if 0 <= t + ahead <= last:
                         op(t + ahead, *args)

@@ -24,12 +24,13 @@ FLOPS = 2 * ROWS * SPLITS * 2 * WIN * WIN * C
 BYTES = 4 * ROWS * SPLITS * WIN * WIN + 2 * 2 * (ROWS * SPLITS * WIN * C) + 2 * SPLITS * WIN * WIN + 4 * ROWS * SPLITS * WIN * C + 4 * SPLITS * WIN * WIN
 
 PE_SUMMED = ((0, 0), (0, 1), (1, 0))
-E_COLS_ON_VECTOR = 256
+E_COLS_ON_VECTOR = (288, 288, 288, 288, 288, 288, 288, 288)
 
+DZ_COLS_ON_VECTOR = (0, 0, 0, 0, 0, 0, 0, 0)
+V_ON_VECTOR = ()
 TURN_BUFS, DE_BUFS, DV_BUFS = 2, 2, 2
 G_FROM = 2
-G_HALF = 1
-WORDS_ON_VECTOR = ()
+G_TILES = 2
 
 
 def tile_single_head_split_window_attention_1d_v_kernel(
@@ -78,13 +79,15 @@ def tile_single_head_split_window_attention_1d_v_kernel(
                     msrc = attn_mask[n].rearrange("(p j) k -> p j k", j=J)
                     nc.sync.dma_start(out=mask[n][:, a : a + J // halves, :], in_=msrc[:, a : a + J // halves, :])
 
-        def late_scores(i):
-            if i > 5:
+        def late_loads(i):
+            if i >= 5:
                 load_scores(i, 1)
+                load_grad(i)
+                load_v(i)
 
         def load_grad(i):
             n, r = steps[i]
-            t = io.tile([P, J, C], BF16, name="g", bufs=8)
+            t = io.tile([P, J, C], BF16, name="g", bufs=5)
             tiles[i]["g"] = t
             for win0, x0, rows in spans(n, r):
                 src = image(grad_out, r)[x0 : x0 + rows, :].rearrange("(p j) c -> p j c", j=J)
@@ -92,18 +95,23 @@ def tile_single_head_split_window_attention_1d_v_kernel(
 
         def load_v(i):
             n, r = steps[i]
-            t = io.tile([P, J, C], BF16, name="v", bufs=8)
+            t = io.tile([P, J, C], BF16, name="v", bufs=5)
             tiles[i]["v"] = t
             for win0, x0, rows in spans(n, r):
                 src = image(v, r)[x0 : x0 + rows, :].rearrange("(t p) c -> p t c", p=P)
                 nc.sync.dma_start(out=t[:, win0 // P : (win0 + rows) // P, :], in_=src)
 
-        def add_mask(i, half):
-            e = tiles[i]["e"]
-            sl = slice(2 * half, 2 * half + 2)
-            for js in [sl] if i < G_FROM or half < G_HALF else [slice(j, j + 1) for j in range(2 * half, 2 * half + 2)]:
-                engine = nc.vector if i < G_FROM or half < G_HALF else nc.gpsimd
-                engine.tensor_tensor(out=e[:, js, :], in0=e[:, js, :], in1=mask[steps[i][0]][:, js, :], op=ADD)
+        def add_mask(i):
+            e, m = tiles[i]["e"], mask[steps[i][0]]
+            mine = J if i < G_FROM else J - G_TILES
+            step = 1 if i == 0 else mine
+            for a in range(0, mine, step):
+                nc.vector.tensor_tensor(out=e[:, a : a + step, :], in0=e[:, a : a + step, :], in1=m[:, a : a + step, :], op=ADD)
+
+        def add_mask_g(i, j):
+            if i >= G_FROM and j >= J - G_TILES:
+                e, m = tiles[i]["e"], mask[steps[i][0]]
+                nc.gpsimd.tensor_tensor(out=e[:, j, :], in0=e[:, j, :], in1=m[:, j, :], op=ADD)
 
         def exponential(i, j):
             if j == 0:
@@ -117,8 +125,12 @@ def tile_single_head_split_window_attention_1d_v_kernel(
             tiles[i]["rz"] = small.tile([P, J], F32, name="rz")
             nc.vector.reciprocal(out=tiles[i]["rz"][:], in_=tiles[i]["z"][:])
 
+        def negate(i):
+            tiles[i]["neg_rz"] = small.tile([P, J], F32, name="neg_rz")
+            nc.gpsimd.tensor_scalar(out=tiles[i]["neg_rz"][:], in0=tiles[i]["rz"][:], scalar1=-1.0, scalar2=0.0, op0=MULT, op1=ADD)
+
         def scale(i):
-            tiles[i]["dz"] = work.tile([P, J, C], BF16, name="dz", align_bytes=64)
+            tiles[i]["dz"] = work.tile([P, J, C], BF16, name="dz", bufs=3, align_bytes=64)
             for j in range(J):
                 nc.vector.tensor_scalar(
                     out=tiles[i]["dz"][:, j, :], in0=tiles[i]["g"][:, j, :], scalar1=tiles[i]["rz"][:, j : j + 1], scalar2=None, op0=MULT
@@ -131,16 +143,24 @@ def tile_single_head_split_window_attention_1d_v_kernel(
             )
 
         def interleave_e_v(i):
-            tiles[i]["e_il"] = work.tile([P, WIN, J], BF16, name="e_il", align_bytes=64)
-            if E_COLS_ON_VECTOR:
-                nc.vector.tensor_copy(**four_by_four(tiles[i]["e_il"], tiles[i]["e"], slice(0, E_COLS_ON_VECTOR)))
+            tiles[i]["ev"] = work.tile([P, 2, WIN, J], BF16, name="ev", bufs=3, align_bytes=64)
+            tiles[i]["e_il"] = tiles[i]["ev"][:, 0]
+            tiles[i]["v_t"] = tiles[i]["ev"][:, 1]
+            if E_COLS_ON_VECTOR[i]:
+                nc.vector.tensor_copy(**four_by_four(tiles[i]["e_il"], tiles[i]["e"], slice(0, E_COLS_ON_VECTOR[i])))
 
         def interleave_e_s(i):
-            nc.scalar.copy(**four_by_four(tiles[i]["e_il"], tiles[i]["e"], slice(E_COLS_ON_VECTOR, WIN)))
+            if E_COLS_ON_VECTOR[i] < WIN:
+                nc.scalar.copy(**four_by_four(tiles[i]["e_il"], tiles[i]["e"], slice(E_COLS_ON_VECTOR[i], WIN)))
 
         def interleave_dz(i):
-            tiles[i]["dz_il"] = work.tile([P, C, J], BF16, name="dz_il", align_bytes=64)
-            nc.scalar.copy(**four_by_four(tiles[i]["dz_il"], tiles[i]["dz"], slice(0, C)))
+            tiles[i]["dz_il"] = work.tile([P, C, J], BF16, name="dz_il", bufs=3, align_bytes=64)
+            if DZ_COLS_ON_VECTOR[i] < C:
+                nc.scalar.copy(**four_by_four(tiles[i]["dz_il"], tiles[i]["dz"], slice(0, C - DZ_COLS_ON_VECTOR[i])))
+
+        def interleave_dz_v(i):
+            if DZ_COLS_ON_VECTOR[i]:
+                nc.vector.tensor_copy(**four_by_four(tiles[i]["dz_il"], tiles[i]["dz"], slice(C - DZ_COLS_ON_VECTOR[i], C)))
 
         def quantise(i, name, src, fmt):
             codes = work.tile([P, 512], U32, name=name + "_q", align_bytes=64)
@@ -148,6 +168,18 @@ def tile_single_head_split_window_attention_1d_v_kernel(
             tiles[i][name + "_q"] = codes[:].bitcast(fmt)
             tiles[i][name + "_s"] = scl
             nc.vector.quantize_mx(out=codes[:].bitcast(fmt), scales=scl[:], in_=tiles[i][src][:].rearrange("p a b -> p (a b)"))
+
+        def quantise_ev(i):
+            codes = work.tile([P, 2, 512], U32, name="ev_q", align_bytes=64)
+            scl = work.tile([P, 2, 512], U8, name="ev_s", align_bytes=64)
+            t = tiles[i]
+            nc.vector.quantize_mx(
+                out=codes[:].rearrange("p o x -> p (o x)").bitcast(E4M3X4),
+                scales=scl[:].rearrange("p o x -> p (o x)"),
+                in_=t["ev"][:].rearrange("p o x j -> p (o x j)"),
+            )
+            t["e_q"], t["e_s"] = codes[:, 0, :].bitcast(E4M3X4), scl[:, 0, :]
+            t["vt_q"], t["vt_s"] = codes[:, 1, :].bitcast(E4M3X4), scl[:, 1, :]
 
         def turn(i, name, b):
             words = tiles[i][name][:].rearrange("p a c -> p (a c)").bitcast(F32).rearrange("p (a c) -> p a c", a=J)
@@ -158,12 +190,12 @@ def tile_single_head_split_window_attention_1d_v_kernel(
                     nc.tensor.transpose(ps[:, a, u, :], words[:, 2 * b + a, u : C // 2 : 2], ident[:])
 
         def unload(i, name, b):
-            if b == 0:
-                tiles[i][name + "_t"] = work.tile([P, WIN, J], BF16, name=name + "_t", align_bytes=64)
+            if b == 0 and name == "dz":
+                tiles[i]["dz_t"] = work.tile([P, WIN, J], BF16, name="dz_t", bufs=3, align_bytes=64)
             words = tiles[i][name + "_t"][:].rearrange("p x j -> p (x j)").bitcast(F32)
             words = words.rearrange("p (b a x u) -> p b a x u", b=2, a=2, u=2)
             src = tiles[i][name, b][:].rearrange("p a u x -> p a x u")
-            if (name, b) in WORDS_ON_VECTOR:
+            if name == "v" and (i, b) in V_ON_VECTOR:
                 nc.vector.tensor_copy(out=words[:, b], in_=src)
             else:
                 nc.scalar.copy(out=words[:, b], in_=src)
@@ -174,7 +206,7 @@ def tile_single_head_split_window_attention_1d_v_kernel(
             t["de", j] = ps
             cols = slice(P * j, P * (j + 1))
             nc.tensor.matmul_mx(
-                out=ps[:], lhsT=t["dzt_q"][:, cols], lhsT_scale=t["dzt_s"][:, cols], rhs=t["vt_q"], rhs_scale=t["vt_s"][:],
+                out=ps[:], lhsT=t["dzt_q"][:, cols], lhsT_scale=t["dzt_s"][:, cols], rhs=t["vt_q"], rhs_scale=t["vt_s"],
                 start=True, stop=True,
             )
 
@@ -212,7 +244,7 @@ def tile_single_head_split_window_attention_1d_v_kernel(
         def factors(i):
             t = tiles[i]
             t["factor"] = small.tile([P, J], F32, name="factor")
-            nc.vector.scalar_tensor_tensor(out=t["factor"][:], in0=t["dot"][:], scalar=-1.0, in1=t["rz"][:], op0=MULT, op1=MULT)
+            nc.gpsimd.tensor_tensor(out=t["factor"][:], in0=t["dot"][:], in1=t["neg_rz"][:], op=MULT)
 
         def diagonals(i):
             t = tiles[i]
@@ -267,73 +299,70 @@ def tile_single_head_split_window_attention_1d_v_kernel(
                 nc.scalar.dma_start(out=rmax[:, a:b, 0:J], in_=src)
             for a, b in ((0, 1), (1, 8)):
                 nc.gpsimd.tensor_scalar(out=neg_max[:, a:b, :], in0=rmax[:, a:b, 0:J], scalar1=-1.0, scalar2=0.0, op0=MULT, op1=ADD)
-            load_scores(0, 2)
-            load_grad(0)
             load_v(0)
-            load_scores(1, 1)
-            load_grad(1)
-            load_v(1)
-            for i in range(2, 6):
+            load_scores(0, 4)
+            load_grad(0)
+            for i in range(1, 5):
                 load_scores(i, 1)
-                load_grad(i)
-                load_v(i)
-            for i in range(6, 8):
                 load_grad(i)
                 load_v(i)
 
             order = (
-                (quantise, -1, "dzt", "dz_t", E5M2X4),
-                (multiply_de, -1, 0),
-                (subtract, -2, 3),
-                (multiply_dv, -2, 2),
-                (multiply_dv, -2, 3),
-                (subtract, -2, 0),
-                (interleave_dz, -1),
-                (interleave_e_v, 0),
-                (multiply_de, -1, 1),
-                (empty_dv, -2, 2),
-                (invert, 0),
-                (unload, 0, "v", 0),
-                (empty_dv, -2, 3),
-                (sum_on_tensor, -2, 0),
-                (accumulate, -2, 0, 2),
-                (empty_sum, -2, 0),
-                (unload, 0, "v", 1),
-                (accumulate, -2, 2, 4),
-                (add_mask, 1, 0),
-                (weigh, -1, 0),
-                (multiply_de, -1, 3),
-                (interleave_e_s, 0),
-                (quantise, -1, "dz", "dz_il", E5M2X4),
-                (weigh, -1, 1),
-                (scale, 0),
-                (multiply_dv, -1, 0),
-                (exponential, 1, 0),
-                (multiply_de, -1, 2),
-                (turn, 0, "dz", 0),
-                (exponential, 1, 1),
-                (weigh, -1, 3),
-                (unload, 0, "dz", 0),
-                (weigh, -1, 2),
-                (late_scores, 2),
-                (add_mask, 1, 1),
+                (late_loads, 3),
+                (multiply_dv, -2, 1),
+                (exponential, 1, 2),
                 (exponential, 1, 3),
                 (turn, 0, "dz", 1),
-                (multiply_dv, -1, 1),
-                (sum_on_tensor, -2, 1),
-                (quantise, 0, "vt", "v_t", E4M3X4),
-                (turn, 1, "v", 0),
+                (empty_dv, -2, 3),
+                (negate, -1),
                 (unload, 0, "dz", 1),
+                (subtract, -2, 3),
+                (add_mask_g, 3, 1),
+                (weigh, -1, 1),
                 (turn, 1, "v", 1),
-                (factors, -1),
-                (exponential, 1, 2),
-                (quantise, 0, "e", "e_il", E4M3X4),
+                (multiply_de, -1, 3),
+                (subtract, -1, 0),
+                (sum_on_tensor, -2, 0),
+                (quantise, -1, "dz", "dz_il", E5M2X4),
+                (empty_dv, -2, 1),
+                (quantise_ev, 0),
+                (sum_on_tensor, -2, 1),
+                (empty_sum, -2, 0),
+                (multiply_dv, -1, 0),
+                (accumulate, -2, 2, 4),
+                (subtract, -2, 1),
+                (invert, 1),
+                (interleave_dz, 0),
+                (interleave_e_v, 1),
+                (interleave_dz_v, -3),
+                (quantise, 0, "dzt", "dz_t", E5M2X4),
+                (turn, 1, "v", 0),
+                (multiply_de, 0, 0),
+                (scale, 1),
+                (multiply_dv, -1, 2),
+                (weigh, -1, 3),
+                (accumulate, -2, 0, 2),
+                (unload, 1, "v", 1),
                 (empty_dv, -1, 0),
-                (subtract, -1, 1),
-                (diagonals, -1),
-                (empty_sum, -3, 1),
+                (unload, 1, "v", 0),
+                (add_mask, 2),
+                (empty_dv, -1, 2),
+                (multiply_de, 0, 2),
+                (interleave_e_s, 1),
+                (turn, 1, "dz", 0),
+                (unload, 1, "dz", 0),
+                (weigh, 0, 0),
+                (exponential, 2, 0),
+                (exponential, 2, 1),
+                (factors, -1),
+                (multiply_dv, -1, 3),
+                (add_mask_g, 3, 2),
+                (multiply_de, 0, 1),
+                (weigh, 0, 2),
                 (subtract, -1, 2),
-                (empty_dv, -1, 1),
+                (diagonals, -1),
+                (add_mask_g, 2, 3),
+                (empty_sum, -3, 1),
             )
             for t in range(-3, last + 4):
                 for op, ahead, *args in order:

@@ -23,14 +23,16 @@ SPLITS = 2
 FLOPS = 2 * ROWS * SPLITS * 2 * WIN * WIN * C
 BYTES = 4 * ROWS * SPLITS * WIN * WIN + 2 * 2 * (ROWS * SPLITS * WIN * C) + 2 * SPLITS * WIN * WIN + 4 * ROWS * SPLITS * WIN * C + 4 * SPLITS * WIN * WIN
 
-PE_SUMMED = ((0, 0), (0, 1), (1, 0))
-E_COLS_ON_VECTOR = (288, 288, 288, 288, 288, 288, 288, 288)
+V_FIRST = False
+SUBTRACT = mybir.AluOpType.subtract
+PE_ROWS = ((4, 4, 4, 0), (3, 3, 3, 0))
+G_ACC_UNTIL = 7
+E_COLS_ON_VECTOR = (384,) * 8
 
 DZ_COLS_ON_VECTOR = (0, 0, 0, 0, 0, 0, 0, 0)
 V_ON_VECTOR = ()
-TURN_BUFS, DE_BUFS, DV_BUFS = 2, 2, 2
-G_FROM = 2
-G_TILES = 2
+BANK_BUFS, DE_BUFS, SUM_BUFS = 3, 2, 3
+G_TILES = (0, 3, 3, 3, 3, 3, 3, 3)
 
 
 def tile_single_head_split_window_attention_1d_v_kernel(
@@ -103,13 +105,13 @@ def tile_single_head_split_window_attention_1d_v_kernel(
 
         def add_mask(i):
             e, m = tiles[i]["e"], mask[steps[i][0]]
-            mine = J if i < G_FROM else J - G_TILES
-            step = 1 if i == 0 else mine
+            mine = J - G_TILES[i]
+            step = 1 if i == 0 else max(mine, 1)
             for a in range(0, mine, step):
                 nc.vector.tensor_tensor(out=e[:, a : a + step, :], in0=e[:, a : a + step, :], in1=m[:, a : a + step, :], op=ADD)
 
         def add_mask_g(i, j):
-            if i >= G_FROM and j >= J - G_TILES:
+            if j >= J - G_TILES[i]:
                 e, m = tiles[i]["e"], mask[steps[i][0]]
                 nc.gpsimd.tensor_tensor(out=e[:, j, :], in0=e[:, j, :], in1=m[:, j, :], op=ADD)
 
@@ -124,10 +126,6 @@ def tile_single_head_split_window_attention_1d_v_kernel(
         def invert(i):
             tiles[i]["rz"] = small.tile([P, J], F32, name="rz")
             nc.vector.reciprocal(out=tiles[i]["rz"][:], in_=tiles[i]["z"][:])
-
-        def negate(i):
-            tiles[i]["neg_rz"] = small.tile([P, J], F32, name="neg_rz")
-            nc.gpsimd.tensor_scalar(out=tiles[i]["neg_rz"][:], in0=tiles[i]["rz"][:], scalar1=-1.0, scalar2=0.0, op0=MULT, op1=ADD)
 
         def scale(i):
             tiles[i]["dz"] = work.tile([P, J, C], BF16, name="dz", bufs=3, align_bytes=64)
@@ -183,7 +181,7 @@ def tile_single_head_split_window_attention_1d_v_kernel(
 
         def turn(i, name, b):
             words = tiles[i][name][:].rearrange("p a c -> p (a c)").bitcast(F32).rearrange("p (a c) -> p a c", a=J)
-            ps = psum.tile([P, 2, 2, P], F32, name="turn", bufs=TURN_BUFS)
+            ps = psum.tile([P, 2, 2, P], F32, name="turn", tag="bank", bufs=BANK_BUFS)
             tiles[i][name, b] = ps
             for a in range(2):
                 for u in range(2):
@@ -212,7 +210,7 @@ def tile_single_head_split_window_attention_1d_v_kernel(
 
         def multiply_dv(i, m):
             t = tiles[i]
-            ps = psum.tile([P, C], F32, name="dv", bufs=DV_BUFS)
+            ps = psum.tile([P, C], F32, name="dv", tag="bank", bufs=BANK_BUFS)
             t["dv", m] = ps
             cols = slice(P * m, P * (m + 1))
             nc.tensor.matmul_mx(
@@ -233,61 +231,52 @@ def tile_single_head_split_window_attention_1d_v_kernel(
 
         def weigh(i, j):
             if j == 0:
-                tiles[i]["prod"] = work.tile([P, J, WIN], F32, name="prod")
+                tiles[i]["ds"] = work.tile([P, J, WIN], F32, name="ds")
                 tiles[i]["dot"] = small.tile([P, J], F32, name="dot")
             t = tiles[i]
+            waste = work.tile([P, WIN], F32, name="waste")
             nc.vector.scalar_tensor_tensor(
-                out=t["prod"][:, j, :], in0=t["de", j][:], scalar=1.0, in1=t["e"][:, j, :], op0=MULT, op1=MULT,
+                out=waste[:], in0=t["de", j][:], scalar=t["rz"][:, j : j + 1], in1=t["e"][:, j, :], op0=MULT, op1=MULT,
                 accum_out=t["dot"][:, j : j + 1],
             )
-
-        def factors(i):
-            t = tiles[i]
-            t["factor"] = small.tile([P, J], F32, name="factor")
-            nc.gpsimd.tensor_tensor(out=t["factor"][:], in0=t["dot"][:], in1=t["neg_rz"][:], op=MULT)
-
-        def diagonals(i):
-            t = tiles[i]
-            for j in range(J):
-                if (steps[i][0], j) in PE_SUMMED:
-                    t["diag", j] = small.tile([P, P], F32, name="diag", bufs=4)
-                    nc.gpsimd.tensor_scalar(out=t["diag", j][:], in0=ident[:], scalar1=t["factor"][:, j : j + 1], scalar2=0.0, op0=MULT, op1=ADD)
-
-        def sum_on_tensor(i, j):
-            n, r = steps[i]
-            t = tiles[i]
-            if (n, j) in PE_SUMMED:
-                if r == 0:
-                    sums[n, j] = psum.tile([P, WIN], F32, name="sum", bufs=2)
-                nc.tensor.matmul(out=sums[n, j][:], lhsT=ident[:], rhs=t["prod"][:, j, :], start=(r == 0), stop=False)
-                nc.tensor.matmul(out=sums[n, j][:], lhsT=t["diag", j][:], rhs=t["e"][:, j, :], start=False, stop=(r == ROWS - 1))
 
         def subtract(i, j):
             n, r = steps[i]
             t = tiles[i]
-            if (n, j) not in PE_SUMMED:
-                dst = acc[n] if r == 0 else t["prod"]
-                nc.vector.scalar_tensor_tensor(
-                    out=dst[:, j, :], in0=t["e"][:, j, :], scalar=t["factor"][:, j : j + 1], in1=t["prod"][:, j, :], op0=MULT, op1=ADD
-                )
+            dst = acc[n] if r == 0 and PE_ROWS[n][j] == 0 else t["ds"]
+            nc.vector.scalar_tensor_tensor(
+                out=dst[:, j, :], in0=t["de", j][:], scalar=t["dot"][:, j : j + 1], in1=t["e"][:, j, :], op0=SUBTRACT, op1=MULT
+            )
 
-        def accumulate(i, a, b):
+        def sum_on_tensor(i, j):
             n, r = steps[i]
-            mine = [j for j in range(a, b) if (n, j) not in PE_SUMMED]
-            if r > 0 and mine:
-                sl = slice(mine[0], b)
-                nc.vector.tensor_tensor(out=acc[n][:, sl, :], in0=acc[n][:, sl, :], in1=tiles[i]["prod"][:, sl, :], op=ADD)
-                if r == ROWS - 1:
-                    store_sum(n, sl)
+            if r < PE_ROWS[n][j]:
+                if r == 0:
+                    sums[n, j] = psum.tile([P, WIN], F32, name="sum", bufs=SUM_BUFS)
+                nc.tensor.matmul(out=sums[n, j][:], lhsT=ident[:], rhs=tiles[i]["ds"][:, j, :], start=(r == 0), stop=(r == PE_ROWS[n][j] - 1))
 
-        def store_sum(n, sl):
-            nc.sync.dma_start(out=out_1[n].rearrange("(p j) k -> p j k", j=J)[:, sl, :], in_=acc[n][:, sl, :])
+        def accumulate(i, j):
+            n, r = steps[i]
+            if PE_ROWS[n][j] == 0 and r > 0:
+                engine = nc.gpsimd if i < G_ACC_UNTIL else nc.vector
+                engine.tensor_tensor(out=acc[n][:, j, :], in0=acc[n][:, j, :], in1=tiles[i]["ds"][:, j, :], op=ADD)
+                if r == ROWS - 1:
+                    store_sum(n, j)
+
+        def store_sum(n, j):
+            nc.sync.dma_start(out=out_1[n].rearrange("(p j) k -> p j k", j=J)[:, j, :], in_=acc[n][:, j, :])
 
         def empty_sum(i, j):
             n, r = steps[i]
-            if r == ROWS - 1 and (n, j) in PE_SUMMED:
+            if r == ROWS - 1 and PE_ROWS[n][j] == ROWS:
                 nc.scalar.copy(out=acc[n][:, j, :], in_=sums[n, j][:])
-                store_sum(n, slice(j, j + 1))
+                store_sum(n, j)
+
+        def merge(i, j):
+            n, r = steps[i]
+            if r == ROWS - 1 and PE_ROWS[n][j] == ROWS - 1:
+                nc.vector.tensor_tensor(out=acc[n][:, j, :], in0=sums[n, j][:], in1=tiles[i]["ds"][:, j, :], op=ADD)
+                store_sum(n, j)
 
         make_identity(nc, ident[:])
         nc.vector.memset(warm[:], 0.0)
@@ -299,8 +288,11 @@ def tile_single_head_split_window_attention_1d_v_kernel(
                 nc.scalar.dma_start(out=rmax[:, a:b, 0:J], in_=src)
             for a, b in ((0, 1), (1, 8)):
                 nc.gpsimd.tensor_scalar(out=neg_max[:, a:b, :], in0=rmax[:, a:b, 0:J], scalar1=-1.0, scalar2=0.0, op0=MULT, op1=ADD)
-            load_v(0)
+            if V_FIRST:
+                load_v(0)
             load_scores(0, 4)
+            if not V_FIRST:
+                load_v(0)
             load_grad(0)
             for i in range(1, 5):
                 load_scores(i, 1)
@@ -308,61 +300,63 @@ def tile_single_head_split_window_attention_1d_v_kernel(
                 load_v(i)
 
             order = (
-                (late_loads, 3),
-                (multiply_dv, -2, 1),
-                (exponential, 1, 2),
-                (exponential, 1, 3),
-                (turn, 0, "dz", 1),
-                (empty_dv, -2, 3),
-                (negate, -1),
-                (unload, 0, "dz", 1),
-                (subtract, -2, 3),
-                (add_mask_g, 3, 1),
-                (weigh, -1, 1),
-                (turn, 1, "v", 1),
-                (multiply_de, -1, 3),
-                (subtract, -1, 0),
-                (sum_on_tensor, -2, 0),
-                (quantise, -1, "dz", "dz_il", E5M2X4),
-                (empty_dv, -2, 1),
-                (quantise_ev, 0),
-                (sum_on_tensor, -2, 1),
-                (empty_sum, -2, 0),
-                (multiply_dv, -1, 0),
-                (accumulate, -2, 2, 4),
-                (subtract, -2, 1),
-                (invert, 1),
-                (interleave_dz, 0),
-                (interleave_e_v, 1),
-                (interleave_dz_v, -3),
-                (quantise, 0, "dzt", "dz_t", E5M2X4),
-                (turn, 1, "v", 0),
+                (sum_on_tensor, -1, 1),
+                (subtract, -1, 3),
+                (sum_on_tensor, -2, 2),
                 (multiply_de, 0, 0),
-                (scale, 1),
-                (multiply_dv, -1, 2),
-                (weigh, -1, 3),
-                (accumulate, -2, 0, 2),
-                (unload, 1, "v", 1),
-                (empty_dv, -1, 0),
+                (late_loads, 3),
+                (interleave_e_v, 1),
                 (unload, 1, "v", 0),
-                (add_mask, 2),
-                (empty_dv, -1, 2),
-                (multiply_de, 0, 2),
-                (interleave_e_s, 1),
-                (turn, 1, "dz", 0),
-                (unload, 1, "dz", 0),
-                (weigh, 0, 0),
-                (exponential, 2, 0),
-                (exponential, 2, 1),
-                (factors, -1),
                 (multiply_dv, -1, 3),
-                (add_mask_g, 3, 2),
+                (empty_sum, -2, 0),
+                (accumulate, -2, 3),
+                (interleave_dz, 0),
                 (multiply_de, 0, 1),
-                (weigh, 0, 2),
-                (subtract, -1, 2),
-                (diagonals, -1),
+                (empty_sum, -1, 1),
+                (turn, 1, "v", 1),
                 (add_mask_g, 2, 3),
-                (empty_sum, -3, 1),
+                (scale, 1),
+                (turn, 1, "dz", 0),
+                (sum_on_tensor, -1, 0),
+                (add_mask, 2),
+                (weigh, 0, 0),
+                (empty_dv, -1, 3),
+                (interleave_e_s, 1),
+                (weigh, 0, 1),
+                (add_mask_g, 2, 2),
+                (add_mask_g, 2, 1),
+                (quantise, 0, "dz", "dz_il", E5M2X4),
+                (turn, 1, "dz", 1),
+                (exponential, 2, 0),
+                (unload, 1, "v", 1),
+                (multiply_dv, 0, 0),
+                (subtract, 0, 0),
+                (unload, 1, "dz", 0),
+                (subtract, 0, 1),
+                (quantise_ev, 1),
+                (exponential, 2, 2),
+                (merge, 0, 0),
+                (unload, 1, "dz", 1),
+                (merge, -1, 2),
+                (multiply_de, 0, 2),
+                (empty_dv, 0, 0),
+                (multiply_dv, 0, 2),
+                (multiply_de, 0, 3),
+                (exponential, 2, 3),
+                (multiply_dv, 0, 1),
+                (merge, 0, 1),
+                (turn, 2, "v", 0),
+                (quantise, 1, "dzt", "dz_t", E5M2X4),
+                (interleave_dz_v, -2),
+                (weigh, 0, 2),
+                (exponential, 2, 1),
+                (empty_sum, -2, 2),
+                (add_mask_g, 2, 0),
+                (empty_dv, 0, 2),
+                (weigh, 0, 3),
+                (empty_dv, 0, 1),
+                (invert, 2),
+                (subtract, 0, 2),
             )
             for t in range(-3, last + 4):
                 for op, ahead, *args in order:

from contextlib import ExitStack

import concourse.mybir as mybir
from concourse.masks import make_identity

F32 = mybir.dt.float32
BF16 = mybir.dt.bfloat16
U32 = mybir.dt.uint32
U8 = mybir.dt.uint8
E4M3X4 = mybir.dt.float8_e4m3fn_x4
E5M2X4 = mybir.dt.float8_e5m2_x4
ADD = mybir.AluOpType.add
MULT = mybir.AluOpType.mult
EXP = mybir.ActivationFunctionType.Exp

P = 128
J = 4
WIN = 512
C = 512
ROWS = 4
SPLITS = 2

FLOPS = 2 * ROWS * SPLITS * 2 * WIN * WIN * C
BYTES = 4 * ROWS * SPLITS * WIN * WIN + 2 * 2 * (ROWS * SPLITS * WIN * C) + 2 * SPLITS * WIN * WIN + 4 * ROWS * SPLITS * WIN * C + 4 * SPLITS * WIN * WIN

V_FIRST = False
SUBTRACT = mybir.AluOpType.subtract
PE_ROWS = ((4, 4, 4, 0), (3, 3, 3, 0))
G_ACC_UNTIL = 7
E_COLS_ON_VECTOR = (384,) * 8

DZ_COLS_ON_VECTOR = (0, 0, 0, 0, 0, 0, 0, 0)
V_ON_VECTOR = ()
BANK_BUFS, DE_BUFS, SUM_BUFS = 3, 2, 3
G_TILES = (0, 3, 3, 3, 3, 3, 3, 3)


def tile_single_head_split_window_attention_1d_v_kernel(
    tc, q, k, v, attn_mask, h, w, num_splits, scores, row_max, grad_out, out_0, out_1
):
    nc = tc.nc
    assert (w, num_splits) == (SPLITS * WIN, SPLITS)
    steps = [(n, r) for n in range(SPLITS) for r in range(ROWS)]
    last = len(steps) - 1

    with ExitStack() as ctx:
        keep = ctx.enter_context(tc.tile_pool(name="keep", bufs=1))
        io = ctx.enter_context(tc.tile_pool(name="io", bufs=1))
        work = ctx.enter_context(tc.tile_pool(name="work", bufs=2))
        small = ctx.enter_context(tc.tile_pool(name="small", bufs=4))
        psum = ctx.enter_context(tc.psum_pool(name="psum", bufs=1))

        ident = keep.tile([P, P], F32, name="ident")
        warm = keep.tile([P, 1], F32, name="warm")
        rmax = keep.tile([P, len(steps), 2 * J], F32, name="rmax")
        neg_max = keep.tile([P, len(steps), J], F32, name="neg_max")
        mask = [keep.tile([P, J, WIN], BF16, name="mask%d" % n) for n in range(SPLITS)]
        acc = [keep.tile([P, J, WIN], F32, name="acc%d" % n) for n in range(SPLITS)]
        tiles = [dict() for s in steps]
        sums = {}

        def image(x, r):
            return x[r // h]

        def spans(n, r):
            first = (r % h) * w
            start = n * WIN + WIN // 2
            if start + WIN <= w:
                return [(0, first + start, WIN)]
            head = w - start
            return [(0, first + start, head), (head, first, WIN - head)]

        def load_scores(i, halves):
            n, r = steps[i]
            t = io.tile([P, J, WIN], F32, name="e", bufs=6)
            tiles[i]["e"] = t
            src = scores[r, n].rearrange("(p j) k -> p j k", j=J)
            for a in range(0, J, J // halves):
                nc.sync.dma_start(out=t[:, a : a + J // halves, :], in_=src[:, a : a + J // halves, :])
                if r == 0:
                    msrc = attn_mask[n].rearrange("(p j) k -> p j k", j=J)
                    nc.sync.dma_start(out=mask[n][:, a : a + J // halves, :], in_=msrc[:, a : a + J // halves, :])

        def late_loads(i):
            if i >= 5:
                load_scores(i, 1)
                load_grad(i)
                load_v(i)

        def load_grad(i):
            n, r = steps[i]
            t = io.tile([P, J, C], BF16, name="g", bufs=5)
            tiles[i]["g"] = t
            for win0, x0, rows in spans(n, r):
                src = image(grad_out, r)[x0 : x0 + rows, :].rearrange("(p j) c -> p j c", j=J)
                nc.sync.dma_start(out=t[win0 // J : (win0 + rows) // J, :, :], in_=src)

        def load_v(i):
            n, r = steps[i]
            t = io.tile([P, J, C], BF16, name="v", bufs=5)
            tiles[i]["v"] = t
            for win0, x0, rows in spans(n, r):
                src = image(v, r)[x0 : x0 + rows, :].rearrange("(t p) c -> p t c", p=P)
                nc.sync.dma_start(out=t[:, win0 // P : (win0 + rows) // P, :], in_=src)

        def add_mask(i):
            e, m = tiles[i]["e"], mask[steps[i][0]]
            mine = J - G_TILES[i]
            step = 1 if i == 0 else max(mine, 1)
            for a in range(0, mine, step):
                nc.vector.tensor_tensor(out=e[:, a : a + step, :], in0=e[:, a : a + step, :], in1=m[:, a : a + step, :], op=ADD)

        def add_mask_g(i, j):
            if j >= J - G_TILES[i]:
                e, m = tiles[i]["e"], mask[steps[i][0]]
                nc.gpsimd.tensor_tensor(out=e[:, j, :], in0=e[:, j, :], in1=m[:, j, :], op=ADD)

        def exponential(i, j):
            if j == 0:
                tiles[i]["z"] = small.tile([P, J], F32, name="z")
            e = tiles[i]["e"]
            nc.scalar.activation(
                out=e[:, j, :], in_=e[:, j, :], func=EXP, bias=neg_max[:, i, j : j + 1], accum_out=tiles[i]["z"][:, j : j + 1]
            )

        def invert(i):
            tiles[i]["rz"] = small.tile([P, J], F32, name="rz")
            nc.vector.reciprocal(out=tiles[i]["rz"][:], in_=tiles[i]["z"][:])

        def scale(i):
            tiles[i]["dz"] = work.tile([P, J, C], BF16, name="dz", bufs=3, align_bytes=64)
            for j in range(J):
                nc.vector.tensor_scalar(
                    out=tiles[i]["dz"][:, j, :], in0=tiles[i]["g"][:, j, :], scalar1=tiles[i]["rz"][:, j : j + 1], scalar2=None, op0=MULT
                )

        def four_by_four(dst, src, cols):
            return dict(
                out=dst[:, cols, :].rearrange("p (c i) j -> p c j i", i=4),
                in_=src[:, :, cols].rearrange("p j (c i) -> p c j i", i=4),
            )

        def interleave_e_v(i):
            tiles[i]["ev"] = work.tile([P, 2, WIN, J], BF16, name="ev", bufs=3, align_bytes=64)
            tiles[i]["e_il"] = tiles[i]["ev"][:, 0]
            tiles[i]["v_t"] = tiles[i]["ev"][:, 1]
            if E_COLS_ON_VECTOR[i]:
                nc.vector.tensor_copy(**four_by_four(tiles[i]["e_il"], tiles[i]["e"], slice(0, E_COLS_ON_VECTOR[i])))

        def interleave_e_s(i):
            if E_COLS_ON_VECTOR[i] < WIN:
                nc.scalar.copy(**four_by_four(tiles[i]["e_il"], tiles[i]["e"], slice(E_COLS_ON_VECTOR[i], WIN)))

        def interleave_dz(i):
            tiles[i]["dz_il"] = work.tile([P, C, J], BF16, name="dz_il", bufs=3, align_bytes=64)
            if DZ_COLS_ON_VECTOR[i] < C:
                nc.scalar.copy(**four_by_four(tiles[i]["dz_il"], tiles[i]["dz"], slice(0, C - DZ_COLS_ON_VECTOR[i])))

        def interleave_dz_v(i):
            if DZ_COLS_ON_VECTOR[i]:
                nc.vector.tensor_copy(**four_by_four(tiles[i]["dz_il"], tiles[i]["dz"], slice(C - DZ_COLS_ON_VECTOR[i], C)))

        def quantise(i, name, src, fmt):
            codes = work.tile([P, 512], U32, name=name + "_q", align_bytes=64)
            scl = work.tile([P, 512], U8, name=name + "_s", align_bytes=64)
            tiles[i][name + "_q"] = codes[:].bitcast(fmt)
            tiles[i][name + "_s"] = scl
            nc.vector.quantize_mx(out=codes[:].bitcast(fmt), scales=scl[:], in_=tiles[i][src][:].rearrange("p a b -> p (a b)"))

        def quantise_ev(i):
            codes = work.tile([P, 2, 512], U32, name="ev_q", align_bytes=64)
            scl = work.tile([P, 2, 512], U8, name="ev_s", align_bytes=64)
            t = tiles[i]
            nc.vector.quantize_mx(
                out=codes[:].rearrange("p o x -> p (o x)").bitcast(E4M3X4),
                scales=scl[:].rearrange("p o x -> p (o x)"),
                in_=t["ev"][:].rearrange("p o x j -> p (o x j)"),
            )
            t["e_q"], t["e_s"] = codes[:, 0, :].bitcast(E4M3X4), scl[:, 0, :]
            t["vt_q"], t["vt_s"] = codes[:, 1, :].bitcast(E4M3X4), scl[:, 1, :]

        def turn(i, name, b):
            words = tiles[i][name][:].rearrange("p a c -> p (a c)").bitcast(F32).rearrange("p (a c) -> p a c", a=J)
            ps = psum.tile([P, 2, 2, P], F32, name="turn", tag="bank", bufs=BANK_BUFS)
            tiles[i][name, b] = ps
            for a in range(2):
                for u in range(2):
                    nc.tensor.transpose(ps[:, a, u, :], words[:, 2 * b + a, u : C // 2 : 2], ident[:])

        def unload(i, name, b):
            if b == 0 and name == "dz":
                tiles[i]["dz_t"] = work.tile([P, WIN, J], BF16, name="dz_t", bufs=3, align_bytes=64)
            words = tiles[i][name + "_t"][:].rearrange("p x j -> p (x j)").bitcast(F32)
            words = words.rearrange("p (b a x u) -> p b a x u", b=2, a=2, u=2)
            src = tiles[i][name, b][:].rearrange("p a u x -> p a x u")
            if name == "v" and (i, b) in V_ON_VECTOR:
                nc.vector.tensor_copy(out=words[:, b], in_=src)
            else:
                nc.scalar.copy(out=words[:, b], in_=src)

        def multiply_de(i, j):
            t = tiles[i]
            ps = psum.tile([P, WIN], F32, name="de", bufs=DE_BUFS)
            t["de", j] = ps
            cols = slice(P * j, P * (j + 1))
            nc.tensor.matmul_mx(
                out=ps[:], lhsT=t["dzt_q"][:, cols], lhsT_scale=t["dzt_s"][:, cols], rhs=t["vt_q"], rhs_scale=t["vt_s"],
                start=True, stop=True,
            )

        def multiply_dv(i, m):
            t = tiles[i]
            ps = psum.tile([P, C], F32, name="dv", tag="bank", bufs=BANK_BUFS)
            t["dv", m] = ps
            cols = slice(P * m, P * (m + 1))
            nc.tensor.matmul_mx(
                out=ps[:], lhsT=t["e_q"][:, cols], lhsT_scale=t["e_s"][:, cols], rhs=t["dz_q"], rhs_scale=t["dz_s"][:],
                start=True, stop=True,
            )

        def empty_dv(i, m):
            n, r = steps[i]
            if m == 0:
                tiles[i]["dv_sb"] = work.tile([P, J, C], F32, name="dv_sb")
            sb = tiles[i]["dv_sb"]
            nc.scalar.copy(out=sb[:, m, :], in_=tiles[i]["dv", m][:])
            if m % 2:
                x0 = [x0 + P * (m - 1) - win0 for win0, x0, rows in spans(n, r) if win0 <= P * (m - 1) < win0 + rows][0]
                dst = image(out_0, r)[x0 : x0 + 2 * P, :].rearrange("(t p) c -> p t c", p=P)
                nc.sync.dma_start(out=dst, in_=sb[:, m - 1 : m + 1, :])

        def weigh(i, j):
            if j == 0:
                tiles[i]["ds"] = work.tile([P, J, WIN], F32, name="ds")
                tiles[i]["dot"] = small.tile([P, J], F32, name="dot")
            t = tiles[i]
            waste = work.tile([P, WIN], F32, name="waste")
            nc.vector.scalar_tensor_tensor(
                out=waste[:], in0=t["de", j][:], scalar=t["rz"][:, j : j + 1], in1=t["e"][:, j, :], op0=MULT, op1=MULT,
                accum_out=t["dot"][:, j : j + 1],
            )

        def subtract(i, j):
            n, r = steps[i]
            t = tiles[i]
            dst = acc[n] if r == 0 and PE_ROWS[n][j] == 0 else t["ds"]
            nc.vector.scalar_tensor_tensor(
                out=dst[:, j, :], in0=t["de", j][:], scalar=t["dot"][:, j : j + 1], in1=t["e"][:, j, :], op0=SUBTRACT, op1=MULT
            )

        def sum_on_tensor(i, j):
            n, r = steps[i]
            if r < PE_ROWS[n][j]:
                if r == 0:
                    sums[n, j] = psum.tile([P, WIN], F32, name="sum", bufs=SUM_BUFS)
                nc.tensor.matmul(out=sums[n, j][:], lhsT=ident[:], rhs=tiles[i]["ds"][:, j, :], start=(r == 0), stop=(r == PE_ROWS[n][j] - 1))

        def accumulate(i, j):
            n, r = steps[i]
            if PE_ROWS[n][j] == 0 and r > 0:
                engine = nc.gpsimd if i < G_ACC_UNTIL else nc.vector
                engine.tensor_tensor(out=acc[n][:, j, :], in0=acc[n][:, j, :], in1=tiles[i]["ds"][:, j, :], op=ADD)
                if r == ROWS - 1:
                    store_sum(n, j)

        def store_sum(n, j):
            nc.sync.dma_start(out=out_1[n].rearrange("(p j) k -> p j k", j=J)[:, j, :], in_=acc[n][:, j, :])

        def empty_sum(i, j):
            n, r = steps[i]
            if r == ROWS - 1 and PE_ROWS[n][j] == ROWS:
                nc.scalar.copy(out=acc[n][:, j, :], in_=sums[n, j][:])
                store_sum(n, j)

        def merge(i, j):
            n, r = steps[i]
            if r == ROWS - 1 and PE_ROWS[n][j] == ROWS - 1:
                nc.vector.tensor_tensor(out=acc[n][:, j, :], in0=sums[n, j][:], in1=tiles[i]["ds"][:, j, :], op=ADD)
                store_sum(n, j)

        make_identity(nc, ident[:])
        nc.vector.memset(warm[:], 0.0)
        nc.scalar.activation(out=warm[:], in_=warm[:], func=EXP)
        with tc.manual_schedule():
            for a, b in ((0, 1), (1, 4), (4, 5), (5, 8)):
                n, r0 = steps[a]
                src = row_max[r0 : r0 + b - a, n].rearrange("r (p j) -> p r j", j=J)
                nc.scalar.dma_start(out=rmax[:, a:b, 0:J], in_=src)
            for a, b in ((0, 1), (1, 8)):
                nc.gpsimd.tensor_scalar(out=neg_max[:, a:b, :], in0=rmax[:, a:b, 0:J], scalar1=-1.0, scalar2=0.0, op0=MULT, op1=ADD)
            if V_FIRST:
                load_v(0)
            load_scores(0, 4)
            if not V_FIRST:
                load_v(0)
            load_grad(0)
            for i in range(1, 5):
                load_scores(i, 1)
                load_grad(i)
                load_v(i)

            order = (
                (sum_on_tensor, -1, 1),
                (subtract, -1, 3),
                (sum_on_tensor, -2, 2),
                (multiply_de, 0, 0),
                (late_loads, 3),
                (interleave_e_v, 1),
                (unload, 1, "v", 0),
                (multiply_dv, -1, 3),
                (empty_sum, -2, 0),
                (accumulate, -2, 3),
                (interleave_dz, 0),
                (multiply_de, 0, 1),
                (empty_sum, -1, 1),
                (turn, 1, "v", 1),
                (add_mask_g, 2, 3),
                (scale, 1),
                (turn, 1, "dz", 0),
                (sum_on_tensor, -1, 0),
                (add_mask, 2),
                (weigh, 0, 0),
                (empty_dv, -1, 3),
                (interleave_e_s, 1),
                (weigh, 0, 1),
                (add_mask_g, 2, 2),
                (add_mask_g, 2, 1),
                (quantise, 0, "dz", "dz_il", E5M2X4),
                (turn, 1, "dz", 1),
                (exponential, 2, 0),
                (unload, 1, "v", 1),
                (multiply_dv, 0, 0),
                (subtract, 0, 0),
                (unload, 1, "dz", 0),
                (subtract, 0, 1),
                (quantise_ev, 1),
                (exponential, 2, 2),
                (merge, 0, 0),
                (unload, 1, "dz", 1),
                (merge, -1, 2),
                (multiply_de, 0, 2),
                (empty_dv, 0, 0),
                (multiply_dv, 0, 2),
                (multiply_de, 0, 3),
                (exponential, 2, 3),
                (multiply_dv, 0, 1),
                (merge, 0, 1),
                (turn, 2, "v", 0),
                (quantise, 1, "dzt", "dz_t", E5M2X4),
                (interleave_dz_v, -2),
                (weigh, 0, 2),
                (exponential, 2, 1),
                (empty_sum, -2, 2),
                (add_mask_g, 2, 0),
                (empty_dv, 0, 2),
                (weigh, 0, 3),
                (empty_dv, 0, 1),
                (invert, 2),
                (subtract, 0, 2),
            )
            for t in range(-3, last + 4):
                for op, ahead, *args in order:
                    if 0 <= t + ahead <= last:
                        op(t + ahead, *args)
